import numpy as np
import ml_dtypes


def mxq(x, axis, fmt="e4m3"):
    dtype, down = {"e4m3": (ml_dtypes.float8_e4m3fn, 7), "e5m2": (ml_dtypes.float8_e5m2, 14)}[fmt]
    v = np.moveaxis(np.asarray(x, np.float32).astype(ml_dtypes.bfloat16).astype(np.float64), axis, -1)
    blocks = v.reshape(v.shape[:-1] + (-1, 32))
    amax = np.abs(blocks).max(-1, keepdims=True)
    byte = np.maximum(np.where(amax > 0, np.frexp(amax)[1] - 1 + 127, 0) - down, 1)
    scale = np.exp2(byte - 127.0)
    codes = (blocks / scale).astype(np.float32).astype(dtype).astype(np.float64)
    return np.moveaxis((codes * scale).reshape(v.shape), -1, axis)


WIDE = False


def mx_kscale(k):
    if not WIDE:
        return np.ones(k)
    levels = np.array([10, -10, 5, -5, 0])
    if k % 512:
        return np.exp2(np.random.permutation(np.resize(levels, k // 32))).repeat(32)
    a = np.empty((k // 512, 16))
    for p in range(k // 512):
        a[p, :8] = np.random.permutation(np.resize(levels, 8))
        for g in range(8):
            far = levels[np.abs(levels - a[p, g]) >= 10]
            a[p, g + 8] = far[np.random.randint(len(far))]
    return np.exp2(a.ravel()).repeat(32)


BF16 = ml_dtypes.bfloat16


def bf(x):
    return np.asarray(x, np.float32).astype(BF16)


def f64(x):
    return np.asarray(x).astype(np.float64)


B, S, HID, NH, NKV, HD, FF = 16, 512, 512, 1, 1, 128, 8192
T = B * S
EPS = 1e-6


def rms(u, w):
    return u * (1.0 / np.sqrt(np.mean(u * u, axis=-1, keepdims=True) + EPS)) * w


def rotate_half(u):
    u1, u2 = np.split(u, 2, axis=-1)
    return np.concatenate([-u2, u1], axis=-1)


def setup_inputs():
    s = mx_kscale(HID)
    pos = np.tile(np.arange(S, dtype=np.float64), B)
    inv_freq = 1.0 / (10000.0 ** (np.arange(0, HD, 2, dtype=np.float64) / HD))
    ang = pos[:, None] * inv_freq[None, :]
    emb = np.concatenate([ang, ang], axis=-1)
    a = 1.0 / np.sqrt(HID)
    return {"x": bf(np.random.standard_normal((T, HID)) * 0.5),
            "cos": bf(np.cos(emb)),
            "sin": bf(np.sin(emb)),
            "wq": bf(np.random.standard_normal((NH * HD, HID)) * a / s[None, :]),
            "bq": bf(np.random.standard_normal(NH * HD) * 0.3),
            "wk": bf(np.random.standard_normal((NKV * HD, HID)) * a / s[None, :]),
            "bk": bf(np.random.standard_normal(NKV * HD) * 0.3),
            "wv": bf(np.random.standard_normal((NKV * HD, HID)) * 2.0 * a / s[None, :]),
            "bv": bf(np.random.standard_normal(NKV * HD) * 0.3),
            "q_norm_w": bf(1.0 + 0.1 * np.random.standard_normal(HD)),
            "k_norm_w": bf(1.0 + 0.1 * np.random.standard_normal(HD)),
            "ln1_w": bf((1.0 + 0.1 * np.random.standard_normal(HID)) * s)}


def reference(x, cos, sin, wq, bq, wk, bk, wv, bv, q_norm_w, k_norm_w, ln1_w):
    h = rms(f64(x), f64(ln1_w))
    hq = mxq(h, 1, "e4m3")
    q = ((hq @ mxq(f64(wq), 1, "e4m3").T) + f64(bq)).reshape(T, NH, HD)
    k = ((hq @ mxq(f64(wk), 1, "e4m3").T) + f64(bk)).reshape(T, NKV, HD)
    v = ((hq @ mxq(f64(wv), 1, "e4m3").T) + f64(bv)).reshape(T, NKV, HD)
    q = rms(q, f64(q_norm_w))
    k = rms(k, f64(k_norm_w))
    c, sn = f64(cos)[:, None, :], f64(sin)[:, None, :]
    q = q * c + rotate_half(q) * sn
    k = k * c + rotate_half(k) * sn
    return q, k, v

@@ -1,0 +1,363 @@
+from contextlib import ExitStack
+
+import concourse.mybir as mybir
+from concourse.masks import make_identity
+
+F32 = mybir.dt.float32
+BF16 = mybir.dt.bfloat16
+U32 = mybir.dt.uint32
+U8 = mybir.dt.uint8
+FP8X4 = mybir.dt.float8_e4m3fn_x4
+ALU = mybir.AluOpType
+ACT = mybir.ActivationFunctionType
+
+P = 128
+TOKENS = 8192
+HID = 512
+HD = 128
+HALF = HD // 2
+EPS = 1e-6
+TILES = 2
+UNIT = TILES * P
+N_UNITS = TOKENS // UNIT
+DEPTH = 6
+WEIGHTS_ROUND = 2
+GAIN_ROWS = HID // P
+
+FLOPS = 2 * TOKENS * HID * 3 * HD
+
+
+def tile_qwen2decoderlayer_pa_t_kernel(
+    tc, x, cos, sin, wq, bq, wk, bk, wv, bv, q_norm_w, k_norm_w, ln1_w, out_0, out_1, out_2
+):
+    nc = tc.nc
+    q_out = out_0.flatten_outer_dims()
+    k_out = out_1.flatten_outer_dims()
+    v_out = out_2.flatten_outer_dims()
+
+    with ExitStack() as ctx:
+        ctx.enter_context(tc.manual_schedule())
+        consts = ctx.enter_context(tc.tile_pool(name="consts", bufs=1))
+        inputs = ctx.enter_context(tc.tile_pool(name="inputs", bufs=N_UNITS))
+        work = ctx.enter_context(tc.tile_pool(name="work", bufs=3))
+        small = ctx.enter_context(tc.tile_pool(name="small", bufs=4))
+        unread = ctx.enter_context(tc.tile_pool(name="unread", bufs=4))
+        results = ctx.enter_context(tc.tile_pool(name="results", bufs=6))
+        psum = ctx.enter_context(tc.psum_pool(name="psum", bufs=2))
+
+        x_of, cos_of, sin_of = {}, {}, {}
+
+        def load_x(u):
+            x_sb = inputs.tile([P, TILES, HID], BF16)
+            nc.sync.dma_start(
+                out=x_sb[:],
+                in_=x[u * UNIT : (u + 1) * UNIT, :].rearrange("(p j) k -> p j k", j=TILES),
+            )
+            x_of[u] = x_sb
+
+        def load_angles(u):
+            rows = slice(u * UNIT, (u + 1) * UNIT)
+            cos_sb = inputs.tile([P, TILES, HD], BF16)
+            nc.sync.dma_start(
+                out=cos_sb[:], in_=cos[rows, :].rearrange("(p j) d -> p j d", j=TILES)
+            )
+            sin_sb = inputs.tile([P, TILES, HD], BF16)
+            nc.sync.dma_start(
+                out=sin_sb[:], in_=sin[rows, :].rearrange("(p j) d -> p j d", j=TILES)
+            )
+            cos_of[u], sin_of[u] = cos_sb, sin_sb
+
+        load_x(0)
+        vector_rows = consts.tile([P, P], BF16)
+        nc.vector.memset(vector_rows[:], 0.0)
+        nc.sync.dma_start(
+            out=vector_rows[0:GAIN_ROWS, :], in_=ln1_w.rearrange("(c k) -> c k", c=GAIN_ROWS)
+        )
+        for head, b in enumerate((bq, bk)):
+            nc.sync.dma_start(
+                out=vector_rows[GAIN_ROWS + head : GAIN_ROWS + head + 1, :],
+                in_=b.rearrange("(o d) -> o d", o=1),
+            )
+        load_x(1)
+        w_rows = consts.tile([P, 3, HID], BF16)
+        for head, w in enumerate((wq, wk, wv)):
+            nc.sync.dma_start(out=w_rows[:, head, :], in_=w)
+        load_x(2)
+        v_bias = consts.tile([P, HD], BF16)
+        nc.sync.dma_start(out=v_bias[:], in_=bv.partition_broadcast(P))
+        head_gain = consts.tile([P, 2, HD], BF16)
+        for head, g in enumerate((q_norm_w, k_norm_w)):
+            nc.sync.dma_start(out=head_gain[:, head, :], in_=g.partition_broadcast(P))
+        for u in range(N_UNITS):
+            if u + 3 < N_UNITS:
+                load_x(u + 3)
+            load_angles(u)
+
+        eps_col = consts.tile([P, 1], F32)
+        nc.vector.memset(eps_col[:], EPS)
+        first_sqrt = consts.tile([P, 1], F32)
+        nc.scalar.activation(out=first_sqrt[:], in_=eps_col[:], func=ACT.Sqrt)
+        ident_f32 = consts.tile([P, P], F32)
+        make_identity(nc, ident_f32[:])
+        ident_bf16 = consts.tile([P, P], BF16)
+        make_identity(nc, ident_bf16[:])
+
+        vectorsT_ps = psum.tile([P, P], BF16, tag="back_qk")
+        nc.tensor.transpose(vectorsT_ps[:], vector_rows[:], ident_bf16[:])
+        vector_cols = consts.tile([P, GAIN_ROWS + 2], F32)
+        nc.vector.tensor_copy(out=vector_cols[:], in_=vectorsT_ps[:, 0 : GAIN_ROWS + 2])
+        bias_col = vector_cols[:, GAIN_ROWS : GAIN_ROWS + 2]
+        ln1_gain = psum.tile([P, HID], F32, bufs=1)
+        for c in range(GAIN_ROWS):
+            nc.tensor.transpose(
+                ln1_gain[:, c * P : (c + 1) * P],
+                vector_cols[:, c : c + 1].to_broadcast([P, P]),
+                ident_f32[:],
+            )
+
+        w_grouped = consts.tile([P, 3, HID], BF16, align_bytes=64)
+        w_codes = consts.tile([P, 3 * HD], U32, align_bytes=64)
+        w_scales = consts.tile([P, 3 * HD], U8, align_bytes=64)
+
+        def prepare_weights():
+            for head in range(3):
+                wT_ps = psum.tile([P, 2, HD], F32, tag="back_qk")
+                for half in range(2):
+                    nc.tensor.transpose(
+                        wT_ps[:, half, :],
+                        w_rows[:, head, :].bitcast(F32)[:, half : 2 * P : 2],
+                        ident_f32[:],
+                    )
+                nc.vector.tensor_copy(
+                    out=w_grouped[:, head, :].bitcast(F32).rearrange("p (d h) -> p d h", h=2),
+                    in_=wT_ps[:].rearrange("p h d -> p d h"),
+                )
+            for head in range(3):
+                cols = slice(head * HD, (head + 1) * HD)
+                nc.vector.quantize_mx(
+                    out=w_codes[:, cols].bitcast(FP8X4),
+                    scales=w_scales[:, cols],
+                    in_=w_grouped[:, head, :],
+                )
+
+        x_ss_of, x_std_of, x_rstd_of, h_of, hT_of, grouped_of = {}, {}, {}, {}, {}, {}
+        codes_of, scales_of, acc_qk_of, v_ps_of, t1T_of, back_of = {}, {}, {}, {}, {}, {}
+        head_ss_of, head_std_of, head_rstd_of, normed_of, cos_ps_of = {}, {}, {}, {}, {}
+
+        def x_sum_of_squares(u):
+            x_ss = small.tile([P, TILES], F32)
+            for j in range(TILES):
+                x_sq = unread.tile([P, HID], BF16)
+                nc.scalar.activation(
+                    out=x_sq[:], in_=x_of[u][:, j, :], func=ACT.Square,
+                    accum_out=x_ss[:, j : j + 1],
+                )
+            x_ss_of[u] = x_ss
+
+        def x_std(u):
+            std = small.tile([P, TILES], F32, name="x_std_sb")
+            nc.scalar.activation(
+                out=std[:], in_=x_ss_of[u][:], func=ACT.Sqrt, bias=eps_col[:], scale=1.0 / HID
+            )
+            x_std_of[u] = std
+
+        def x_rstd(u):
+            rstd = small.tile([P, TILES], F32, name="x_rstd_sb")
+            nc.vector.reciprocal(out=rstd[:], in_=x_std_of[u][:])
+            x_rstd_of[u] = rstd
+
+        def first_norm(u):
+            h_sb = work.tile([P, TILES, HID], BF16)
+            for j in range(TILES):
+                nc.vector.scalar_tensor_tensor(
+                    out=h_sb[:, j, :], in0=x_of[u][:, j, :], scalar=x_rstd_of[u][:, j : j + 1],
+                    in1=ln1_gain[:], op0=ALU.mult, op1=ALU.mult,
+                )
+            h_of[u] = h_sb
+
+        def h_transposes(u):
+            hT_ps = psum.tile([P, TILES, 2, P], F32, bufs=1)
+            for j in range(TILES):
+                for half in range(2):
+                    nc.tensor.transpose(
+                        hT_ps[:, j, half, :],
+                        h_of[u][:, j, :].bitcast(F32)[:, half : 2 * P : 2],
+                        ident_f32[:],
+                    )
+            hT_of[u] = hT_ps
+
+        def h_regroup(u):
+            h_grouped = work.tile([P, UNIT * 4], BF16, align_bytes=64)
+            nc.scalar.copy(
+                out=h_grouped[:].bitcast(F32).rearrange("p (j t h) -> p j t h", j=TILES, h=2),
+                in_=hT_of[u][:].rearrange("p j h t -> p j t h"),
+            )
+            grouped_of[u] = h_grouped
+
+        def h_quantise(u):
+            h_codes = work.tile([P, UNIT], U32, align_bytes=64)
+            h_scales = work.tile([P, UNIT], U8, align_bytes=64)
+            nc.vector.quantize_mx(
+                out=h_codes[:].bitcast(FP8X4), scales=h_scales[:], in_=grouped_of[u][:]
+            )
+            codes_of[u], scales_of[u] = h_codes, h_scales
+
+        def projections(u):
+            acc_qk = psum.tile([P, 2, UNIT], F32)
+            for head in range(2):
+                cols = slice(head * HD, (head + 1) * HD)
+                nc.tensor.matmul_mx(
+                    out=acc_qk[:, head, :],
+                    lhsT=w_codes[:, cols].bitcast(FP8X4), lhsT_scale=w_scales[:, cols],
+                    rhs=codes_of[u][:].bitcast(FP8X4), rhs_scale=scales_of[u][:],
+                    start=True, stop=True,
+                )
+            v_ps = psum.tile([P, TILES, HD], F32, bufs=1)
+            v_cols = slice(2 * HD, 3 * HD)
+            for j in range(TILES):
+                tok = slice(j * P, (j + 1) * P)
+                nc.tensor.matmul_mx(
+                    out=v_ps[:, j, :],
+                    lhsT=codes_of[u][:, tok].bitcast(FP8X4), lhsT_scale=scales_of[u][:, tok],
+                    rhs=w_codes[:, v_cols].bitcast(FP8X4), rhs_scale=w_scales[:, v_cols],
+                    start=True, stop=True,
+                )
+            acc_qk_of[u], v_ps_of[u] = acc_qk, v_ps
+
+        def finish_v(u):
+            v_sb = results.tile([P, TILES, HD], F32)
+            nc.vector.tensor_tensor(
+                out=v_sb[:], in0=v_ps_of[u][:],
+                in1=v_bias[:].unsqueeze(1).to_broadcast([P, TILES, HD]), op=ALU.add,
+            )
+            nc.sync.dma_start(
+                out=v_out[u * UNIT : (u + 1) * UNIT, :].rearrange("(p j) d -> p j d", j=TILES),
+                in_=v_sb[:],
+            )
+
+        def add_biases(u):
+            t1T = work.tile([P, 2, UNIT], F32)
+            for head in range(2):
+                nc.scalar.activation(
+                    out=t1T[:, head, :], in_=acc_qk_of[u][:, head, :], func=ACT.Identity,
+                    bias=bias_col[:, head : head + 1],
+                )
+            t1T_of[u] = t1T
+
+        def turn_back(u):
+            back_qk = psum.tile([P, 2, TILES, HD], F32)
+            for head in range(2):
+                for j in range(TILES):
+                    nc.tensor.transpose(
+                        back_qk[:, head, j, :], t1T_of[u][:, head, j * P : (j + 1) * P],
+                        ident_f32[:],
+                    )
+            back_of[u] = back_qk
+
+        def head_sums_of_squares(u):
+            head_ss = small.tile([P, 2, TILES], F32)
+            for head in range(2):
+                for j in range(TILES):
+                    head_sq = unread.tile([P, HD], BF16)
+                    nc.scalar.activation(
+                        out=head_sq[:], in_=back_of[u][:, head, j, :], func=ACT.Square,
+                        accum_out=head_ss[:, head, j : j + 1],
+                    )
+            head_ss_of[u] = head_ss
+
+        def head_std(u):
+            std = small.tile([P, 2, TILES], F32, name="head_std_sb")
+            nc.scalar.activation(
+                out=std[:], in_=head_ss_of[u][:], func=ACT.Sqrt, bias=eps_col[:], scale=1.0 / HD
+            )
+            head_std_of[u] = std
+
+        def head_rstd(u):
+            rstd = small.tile([P, 2, TILES], F32, name="head_rstd_sb")
+            nc.vector.reciprocal(out=rstd[:], in_=head_std_of[u][:])
+            head_rstd_of[u] = rstd
+
+        def head_norm(u):
+            normed = work.tile([P, 2, TILES, HD], F32)
+            for head in range(2):
+                for j in range(TILES):
+                    nc.vector.scalar_tensor_tensor(
+                        out=normed[:, head, j, :], in0=back_of[u][:, head, j, :],
+                        scalar=head_rstd_of[u][:, head, j : j + 1], in1=head_gain[:, head, :],
+                        op0=ALU.mult, op1=ALU.mult,
+                    )
+            normed_of[u] = normed
+
+        def cos_to_psum(u):
+            cos_ps = psum.tile([P, TILES, HD], F32, bufs=1)
+            nc.tensor.matmul(
+                out=cos_ps[:], lhsT=ident_bf16[:], rhs=cos_of[u][:], start=True, stop=True
+            )
+            cos_ps_of[u] = cos_ps
+
+        def rope(u):
+            normed = normed_of[u]
+            lo, hi = slice(0, HALF), slice(HALF, HD)
+            both = [P, 2, TILES, HD]
+            both_half = [P, 2, TILES, HALF]
+            crossed = work.tile(both, F32)
+            for here, there in ((lo, hi), (hi, lo)):
+                nc.gpsimd.tensor_tensor(
+                    out=crossed[:, :, :, here], in0=normed[:, :, :, there],
+                    in1=sin_of[u][:, :, here].unsqueeze(1).to_broadcast(both_half), op=ALU.mult,
+                )
+            direct = work.tile(both, F32)
+            nc.vector.tensor_tensor(
+                out=direct[:], in0=cos_ps_of[u][:].unsqueeze(1).to_broadcast(both), in1=normed[:],
+                op=ALU.mult,
+            )
+            qk_sb = results.tile(both, F32)
+            for here, op in ((lo, ALU.subtract), (hi, ALU.add)):
+                nc.gpsimd.tensor_tensor(
+                    out=qk_sb[:, :, :, here], in0=direct[:, :, :, here],
+                    in1=crossed[:, :, :, here], op=op,
+                )
+            rows = slice(u * UNIT, (u + 1) * UNIT)
+            for head, out in enumerate((q_out, k_out)):
+                nc.sync.dma_start(
+                    out=out[rows, :].rearrange("(p j) d -> p j d", j=TILES),
+                    in_=qk_sb[:, head, :, :],
+                )
+
+        def live(u):
+            return 0 <= u < N_UNITS
+
+        for r in range(N_UNITS + DEPTH):
+            if r == WEIGHTS_ROUND:
+                prepare_weights()
+            if live(r - 5):
+                head_sums_of_squares(r - 5)
+            if live(r - 1):
+                x_rstd(r - 1)
+            if live(r - 3):
+                h_quantise(r - 3)
+            if live(r - 4):
+                finish_v(r - 4)
+            if live(r - 3):
+                projections(r - 3)
+            if live(r - 6):
+                rope(r - 6)
+            if live(r - 5):
+                cos_to_psum(r - 5)
+            if live(r - 4):
+                add_biases(r - 4)
+                turn_back(r - 4)
+            if live(r - 5):
+                head_std(r - 5)
+                head_rstd(r - 5)
+            if live(r):
+                x_sum_of_squares(r)
+            if live(r - 2):
+                h_regroup(r - 2)
+            if live(r):
+                x_std(r)
+            if live(r - 1):
+                first_norm(r - 1)
+                h_transposes(r - 1)
+            if live(r - 5):
+                head_norm(r - 5)

@@ -20,9 +20,11 @@ EPS = 1e-6
 TILES = 2
 UNIT = TILES * P
 N_UNITS = TOKENS // UNIT
-DEPTH = 6
+DEPTH = 5
 WEIGHTS_ROUND = 2
+LOAD_AHEAD = 8
 GAIN_ROWS = HID // P
+SUM_COLS = 64
 
 FLOPS = 2 * TOKENS * HID * 3 * HD
 
@@ -73,10 +75,10 @@ def tile_qwen2decoderlayer_pa_t_kernel(
         nc.sync.dma_start(
             out=vector_rows[0:GAIN_ROWS, :], in_=ln1_w.rearrange("(c k) -> c k", c=GAIN_ROWS)
         )
-        for head, b in enumerate((bq, bk)):
+        for row, vec in enumerate((bq, bk, q_norm_w, k_norm_w)):
             nc.sync.dma_start(
-                out=vector_rows[GAIN_ROWS + head : GAIN_ROWS + head + 1, :],
-                in_=b.rearrange("(o d) -> o d", o=1),
+                out=vector_rows[GAIN_ROWS + row : GAIN_ROWS + row + 1, :],
+                in_=vec.rearrange("(o d) -> o d", o=1),
             )
         load_x(1)
         w_rows = consts.tile([P, 3, HID], BF16)
@@ -85,10 +87,7 @@ def tile_qwen2decoderlayer_pa_t_kernel(
         load_x(2)
         v_bias = consts.tile([P, HD], BF16)
         nc.sync.dma_start(out=v_bias[:], in_=bv.partition_broadcast(P))
-        head_gain = consts.tile([P, 2, HD], BF16)
-        for head, g in enumerate((q_norm_w, k_norm_w)):
-            nc.sync.dma_start(out=head_gain[:, head, :], in_=g.partition_broadcast(P))
-        for u in range(N_UNITS):
+        for u in range(LOAD_AHEAD):
             if u + 3 < N_UNITS:
                 load_x(u + 3)
             load_angles(u)
@@ -104,9 +103,16 @@ def tile_qwen2decoderlayer_pa_t_kernel(
 
         vectorsT_ps = psum.tile([P, P], BF16, tag="back_qk")
         nc.tensor.transpose(vectorsT_ps[:], vector_rows[:], ident_bf16[:])
-        vector_cols = consts.tile([P, GAIN_ROWS + 2], F32)
-        nc.vector.tensor_copy(out=vector_cols[:], in_=vectorsT_ps[:, 0 : GAIN_ROWS + 2])
+        vector_cols = consts.tile([P, GAIN_ROWS + 4], F32)
+        nc.vector.tensor_copy(out=vector_cols[:], in_=vectorsT_ps[:, 0 : GAIN_ROWS + 4])
         bias_col = vector_cols[:, GAIN_ROWS : GAIN_ROWS + 2]
+        gain_col = vector_cols[:, GAIN_ROWS + 2 : GAIN_ROWS + 4]
+        gained_bias_col = consts.tile([P, 2], F32)
+        nc.vector.tensor_tensor(
+            out=gained_bias_col[:], in0=bias_col, in1=gain_col, op=ALU.mult
+        )
+        ones = consts.tile([P, SUM_COLS], F32)
+        nc.vector.memset(ones[:], 1.0)
         ln1_gain = psum.tile([P, HID], F32, bufs=1)
         for c in range(GAIN_ROWS):
             nc.tensor.transpose(
@@ -141,8 +147,9 @@ def tile_qwen2decoderlayer_pa_t_kernel(
                 )
 
         x_ss_of, x_std_of, x_rstd_of, h_of, hT_of, grouped_of = {}, {}, {}, {}, {}, {}
-        codes_of, scales_of, acc_qk_of, v_ps_of, t1T_of, back_of = {}, {}, {}, {}, {}, {}
-        head_ss_of, head_std_of, head_rstd_of, normed_of, cos_ps_of = {}, {}, {}, {}, {}
+        codes_of, scales_of, acc_qk_of, v_ps_of, back_of = {}, {}, {}, {}, {}
+        gainedT_of, squaredT_of, head_ss_of, head_std_of, head_rstd_of = {}, {}, {}, {}, {}
+        direct_of, crossed_of = {}, {}
 
         def x_sum_of_squares(u):
             x_ss = small.tile([P, TILES], F32)
@@ -235,40 +242,44 @@ def tile_qwen2decoderlayer_pa_t_kernel(
                 in_=v_sb[:],
             )
 
-        def add_biases(u):
-            t1T = work.tile([P, 2, UNIT], F32)
+        def heads_out_of_psum(u):
+            gainedT = work.tile([P, 2, UNIT], F32)
+            squaredT = work.tile([P, 2, UNIT], F32)
             for head in range(2):
                 nc.scalar.activation(
-                    out=t1T[:, head, :], in_=acc_qk_of[u][:, head, :], func=ACT.Identity,
+                    out=gainedT[:, head, :], in_=acc_qk_of[u][:, head, :], func=ACT.Identity,
+                    scale=gain_col[:, head : head + 1], bias=gained_bias_col[:, head : head + 1],
+                )
+                nc.scalar.activation(
+                    out=squaredT[:, head, :], in_=acc_qk_of[u][:, head, :], func=ACT.Square,
                     bias=bias_col[:, head : head + 1],
                 )
-            t1T_of[u] = t1T
+            gainedT_of[u], squaredT_of[u] = gainedT, squaredT
 
         def turn_back(u):
             back_qk = psum.tile([P, 2, TILES, HD], F32)
             for head in range(2):
                 for j in range(TILES):
                     nc.tensor.transpose(
-                        back_qk[:, head, j, :], t1T_of[u][:, head, j * P : (j + 1) * P],
+                        back_qk[:, head, j, :], gainedT_of[u][:, head, j * P : (j + 1) * P],
                         ident_f32[:],
                     )
             back_of[u] = back_qk
-
-        def head_sums_of_squares(u):
-            head_ss = small.tile([P, 2, TILES], F32)
+            head_ss = psum.tile([P, 2, TILES, SUM_COLS], F32, bufs=1)
             for head in range(2):
                 for j in range(TILES):
-                    head_sq = unread.tile([P, HD], BF16)
-                    nc.scalar.activation(
-                        out=head_sq[:], in_=back_of[u][:, head, j, :], func=ACT.Square,
-                        accum_out=head_ss[:, head, j : j + 1],
+                    nc.tensor.matmul(
+                        out=head_ss[:, head, j, :],
+                        lhsT=squaredT_of[u][:, head, j * P : (j + 1) * P], rhs=ones[:],
+                        start=True, stop=True,
                     )
             head_ss_of[u] = head_ss
 
         def head_std(u):
             std = small.tile([P, 2, TILES], F32, name="head_std_sb")
             nc.scalar.activation(
-                out=std[:], in_=head_ss_of[u][:], func=ACT.Sqrt, bias=eps_col[:], scale=1.0 / HD
+                out=std[:], in_=head_ss_of[u][:, :, :, 0], func=ACT.Sqrt, bias=eps_col[:],
+                scale=1.0 / HD,
             )
             head_std_of[u] = std
 
@@ -277,41 +288,30 @@ def tile_qwen2decoderlayer_pa_t_kernel(
             nc.vector.reciprocal(out=rstd[:], in_=head_std_of[u][:])
             head_rstd_of[u] = rstd
 
-        def head_norm(u):
-            normed = work.tile([P, 2, TILES, HD], F32)
+        def rope_products(u):
+            both = [P, 2, TILES, HD]
+            direct = work.tile(both, F32)
+            crossed = work.tile(both, F32)
             for head in range(2):
                 for j in range(TILES):
+                    rstd = head_rstd_of[u][:, head, j : j + 1]
                     nc.vector.scalar_tensor_tensor(
-                        out=normed[:, head, j, :], in0=back_of[u][:, head, j, :],
-                        scalar=head_rstd_of[u][:, head, j : j + 1], in1=head_gain[:, head, :],
+                        out=direct[:, head, j, :], in0=back_of[u][:, head, j, :], scalar=rstd,
+                        in1=cos_of[u][:, j, :], op0=ALU.mult, op1=ALU.mult,
+                    )
+                    nc.vector.scalar_tensor_tensor(
+                        out=crossed[:, head, j, :].rearrange("p (s d) -> p s d", s=2),
+                        in0=back_of[u][:, head, j, :].rearrange("p (s d) -> p s d", s=2)[:, ::-1, :],
+                        scalar=rstd,
+                        in1=sin_of[u][:, j, :].rearrange("p (s d) -> p s d", s=2),
                         op0=ALU.mult, op1=ALU.mult,
                     )
-            normed_of[u] = normed
+            direct_of[u], crossed_of[u] = direct, crossed
 
-        def cos_to_psum(u):
-            cos_ps = psum.tile([P, TILES, HD], F32, bufs=1)
-            nc.tensor.matmul(
-                out=cos_ps[:], lhsT=ident_bf16[:], rhs=cos_of[u][:], start=True, stop=True
-            )
-            cos_ps_of[u] = cos_ps
-
-        def rope(u):
-            normed = normed_of[u]
+        def rope_sum(u):
+            direct, crossed = direct_of[u], crossed_of[u]
             lo, hi = slice(0, HALF), slice(HALF, HD)
-            both = [P, 2, TILES, HD]
-            both_half = [P, 2, TILES, HALF]
-            crossed = work.tile(both, F32)
-            for here, there in ((lo, hi), (hi, lo)):
-                nc.gpsimd.tensor_tensor(
-                    out=crossed[:, :, :, here], in0=normed[:, :, :, there],
-                    in1=sin_of[u][:, :, here].unsqueeze(1).to_broadcast(both_half), op=ALU.mult,
-                )
-            direct = work.tile(both, F32)
-            nc.vector.tensor_tensor(
-                out=direct[:], in0=cos_ps_of[u][:].unsqueeze(1).to_broadcast(both), in1=normed[:],
-                op=ALU.mult,
-            )
-            qk_sb = results.tile(both, F32)
+            qk_sb = results.tile([P, 2, TILES, HD], F32)
             for here, op in ((lo, ALU.subtract), (hi, ALU.add)):
                 nc.gpsimd.tensor_tensor(
                     out=qk_sb[:, :, :, here], in0=direct[:, :, :, here],
@@ -328,28 +328,24 @@ def tile_qwen2decoderlayer_pa_t_kernel(
             return 0 <= u < N_UNITS
 
         for r in range(N_UNITS + DEPTH):
+            if r + LOAD_AHEAD + 3 < N_UNITS:
+                load_x(r + LOAD_AHEAD + 3)
+            if r + LOAD_AHEAD < N_UNITS:
+                load_angles(r + LOAD_AHEAD)
             if r == WEIGHTS_ROUND:
                 prepare_weights()
-            if live(r - 5):
-                head_sums_of_squares(r - 5)
             if live(r - 1):
                 x_rstd(r - 1)
             if live(r - 3):
                 h_quantise(r - 3)
-            if live(r - 4):
-                finish_v(r - 4)
-            if live(r - 3):
                 projections(r - 3)
-            if live(r - 6):
-                rope(r - 6)
-            if live(r - 5):
-                cos_to_psum(r - 5)
-            if live(r - 4):
-                add_biases(r - 4)
-                turn_back(r - 4)
             if live(r - 5):
                 head_std(r - 5)
                 head_rstd(r - 5)
+            if live(r - 4):
+                heads_out_of_psum(r - 4)
+                turn_back(r - 4)
+                finish_v(r - 4)
             if live(r):
                 x_sum_of_squares(r)
             if live(r - 2):
@@ -360,4 +356,5 @@ def tile_qwen2decoderlayer_pa_t_kernel(
                 first_norm(r - 1)
                 h_transposes(r - 1)
             if live(r - 5):
-                head_norm(r - 5)
+                rope_products(r - 5)
+                rope_sum(r - 5)

@@ -21,7 +21,6 @@ TILES = 2
 UNIT = TILES * P
 N_UNITS = TOKENS // UNIT
 DEPTH = 5
-WEIGHTS_ROUND = 2
 LOAD_AHEAD = 8
 GAIN_ROWS = HID // P
 SUM_COLS = 64
@@ -80,10 +79,10 @@ def tile_qwen2decoderlayer_pa_t_kernel(
                 out=vector_rows[GAIN_ROWS + row : GAIN_ROWS + row + 1, :],
                 in_=vec.rearrange("(o d) -> o d", o=1),
             )
-        load_x(1)
         w_rows = consts.tile([P, 3, HID], BF16)
         for head, w in enumerate((wq, wk, wv)):
             nc.sync.dma_start(out=w_rows[:, head, :], in_=w)
+        load_x(1)
         load_x(2)
         v_bias = consts.tile([P, HD], BF16)
         nc.sync.dma_start(out=v_bias[:], in_=bv.partition_broadcast(P))
@@ -94,8 +93,8 @@ def tile_qwen2decoderlayer_pa_t_kernel(
 
         eps_col = consts.tile([P, 1], F32)
         nc.vector.memset(eps_col[:], EPS)
-        first_sqrt = consts.tile([P, 1], F32)
-        nc.scalar.activation(out=first_sqrt[:], in_=eps_col[:], func=ACT.Sqrt)
+        first_root = consts.tile([P, 1], F32)
+        nc.scalar.activation(out=first_root[:], in_=eps_col[:], func=ACT.Abs_reciprocal_sqrt)
         ident_f32 = consts.tile([P, P], F32)
         make_identity(nc, ident_f32[:])
         ident_bf16 = consts.tile([P, P], BF16)
@@ -146,9 +145,9 @@ def tile_qwen2decoderlayer_pa_t_kernel(
                     in_=w_grouped[:, head, :],
                 )
 
-        x_ss_of, x_std_of, x_rstd_of, h_of, hT_of, grouped_of = {}, {}, {}, {}, {}, {}
+        x_ss_of, x_rstd_of, h_of, hT_of, grouped_of = {}, {}, {}, {}, {}
         codes_of, scales_of, acc_qk_of, v_ps_of, back_of = {}, {}, {}, {}, {}
-        gainedT_of, squaredT_of, head_ss_of, head_std_of, head_rstd_of = {}, {}, {}, {}, {}
+        gainedT_of, squaredT_of, head_ss_of, head_rstd_of = {}, {}, {}, {}
         direct_of, crossed_of = {}, {}
 
         def x_sum_of_squares(u):
@@ -161,16 +160,12 @@ def tile_qwen2decoderlayer_pa_t_kernel(
                 )
             x_ss_of[u] = x_ss
 
-        def x_std(u):
-            std = small.tile([P, TILES], F32, name="x_std_sb")
-            nc.scalar.activation(
-                out=std[:], in_=x_ss_of[u][:], func=ACT.Sqrt, bias=eps_col[:], scale=1.0 / HID
-            )
-            x_std_of[u] = std
-
         def x_rstd(u):
             rstd = small.tile([P, TILES], F32, name="x_rstd_sb")
-            nc.vector.reciprocal(out=rstd[:], in_=x_std_of[u][:])
+            nc.scalar.activation(
+                out=rstd[:], in_=x_ss_of[u][:], func=ACT.Abs_reciprocal_sqrt, bias=eps_col[:],
+                scale=1.0 / HID,
+            )
             x_rstd_of[u] = rstd
 
         def first_norm(u):
@@ -275,17 +270,12 @@ def tile_qwen2decoderlayer_pa_t_kernel(
                     )
             head_ss_of[u] = head_ss
 
-        def head_std(u):
-            std = small.tile([P, 2, TILES], F32, name="head_std_sb")
-            nc.scalar.activation(
-                out=std[:], in_=head_ss_of[u][:, :, :, 0], func=ACT.Sqrt, bias=eps_col[:],
-                scale=1.0 / HD,
-            )
-            head_std_of[u] = std
-
         def head_rstd(u):
             rstd = small.tile([P, 2, TILES], F32, name="head_rstd_sb")
-            nc.vector.reciprocal(out=rstd[:], in_=head_std_of[u][:])
+            nc.scalar.activation(
+                out=rstd[:], in_=head_ss_of[u][:, :, :, 0], func=ACT.Abs_reciprocal_sqrt,
+                bias=eps_col[:], scale=1.0 / HD,
+            )
             head_rstd_of[u] = rstd
 
         def rope_products(u):
@@ -324,6 +314,8 @@ def tile_qwen2decoderlayer_pa_t_kernel(
                     in_=qk_sb[:, head, :, :],
                 )
 
+        prepare_weights()
+
         def live(u):
             return 0 <= u < N_UNITS
 
@@ -332,26 +324,24 @@ def tile_qwen2decoderlayer_pa_t_kernel(
                 load_x(r + LOAD_AHEAD + 3)
             if r + LOAD_AHEAD < N_UNITS:
                 load_angles(r + LOAD_AHEAD)
-            if r == WEIGHTS_ROUND:
-                prepare_weights()
-            if live(r - 1):
-                x_rstd(r - 1)
             if live(r - 3):
                 h_quantise(r - 3)
+            if live(r - 4):
+                finish_v(r - 4)
+            if live(r - 3):
                 projections(r - 3)
-            if live(r - 5):
-                head_std(r - 5)
-                head_rstd(r - 5)
             if live(r - 4):
                 heads_out_of_psum(r - 4)
+            if live(r - 5):
+                head_rstd(r - 5)
+            if live(r - 4):
                 turn_back(r - 4)
-                finish_v(r - 4)
             if live(r):
                 x_sum_of_squares(r)
             if live(r - 2):
                 h_regroup(r - 2)
             if live(r):
-                x_std(r)
+                x_rstd(r)
             if live(r - 1):
                 first_norm(r - 1)
                 h_transposes(r - 1)

@@ -21,6 +21,7 @@ TILES = 2
 UNIT = TILES * P
 N_UNITS = TOKENS // UNIT
 DEPTH = 5
+WEIGHTS_ROUND = 1
 LOAD_AHEAD = 8
 GAIN_ROWS = HID // P
 SUM_COLS = 64
@@ -46,7 +47,7 @@ def tile_qwen2decoderlayer_pa_t_kernel(
         results = ctx.enter_context(tc.tile_pool(name="results", bufs=6))
         psum = ctx.enter_context(tc.psum_pool(name="psum", bufs=2))
 
-        x_of, cos_of, sin_of = {}, {}, {}
+        x_of, angles_of = {}, {}
 
         def load_x(u):
             x_sb = inputs.tile([P, TILES, HID], BF16)
@@ -58,15 +59,16 @@ def tile_qwen2decoderlayer_pa_t_kernel(
 
         def load_angles(u):
             rows = slice(u * UNIT, (u + 1) * UNIT)
-            cos_sb = inputs.tile([P, TILES, HD], BF16)
-            nc.sync.dma_start(
-                out=cos_sb[:], in_=cos[rows, :].rearrange("(p j) d -> p j d", j=TILES)
-            )
-            sin_sb = inputs.tile([P, TILES, HD], BF16)
-            nc.sync.dma_start(
-                out=sin_sb[:], in_=sin[rows, :].rearrange("(p j) d -> p j d", j=TILES)
-            )
-            cos_of[u], sin_of[u] = cos_sb, sin_sb
+            angles = inputs.tile([P, TILES, 2 * HD], BF16)
+            for first, table, columns in (
+                (0, cos, slice(0, HD)), (HD, sin, slice(HALF, HD)), (HD + HALF, sin, slice(0, HALF))
+            ):
+                width = columns.stop - columns.start
+                nc.sync.dma_start(
+                    out=angles[:, :, first : first + width],
+                    in_=table[rows, columns].rearrange("(p j) d -> p j d", j=TILES),
+                )
+            angles_of[u] = angles
 
         load_x(0)
         vector_rows = consts.tile([P, P], BF16)
@@ -79,10 +81,10 @@ def tile_qwen2decoderlayer_pa_t_kernel(
                 out=vector_rows[GAIN_ROWS + row : GAIN_ROWS + row + 1, :],
                 in_=vec.rearrange("(o d) -> o d", o=1),
             )
+        load_x(1)
         w_rows = consts.tile([P, 3, HID], BF16)
         for head, w in enumerate((wq, wk, wv)):
             nc.sync.dma_start(out=w_rows[:, head, :], in_=w)
-        load_x(1)
         load_x(2)
         v_bias = consts.tile([P, HD], BF16)
         nc.sync.dma_start(out=v_bias[:], in_=bv.partition_broadcast(P))
@@ -100,7 +102,7 @@ def tile_qwen2decoderlayer_pa_t_kernel(
         ident_bf16 = consts.tile([P, P], BF16)
         make_identity(nc, ident_bf16[:])
 
-        vectorsT_ps = psum.tile([P, P], BF16, tag="back_qk")
+        vectorsT_ps = psum.tile([P, P], BF16, tag="acc_qk")
         nc.tensor.transpose(vectorsT_ps[:], vector_rows[:], ident_bf16[:])
         vector_cols = consts.tile([P, GAIN_ROWS + 4], F32)
         nc.vector.tensor_copy(out=vector_cols[:], in_=vectorsT_ps[:, 0 : GAIN_ROWS + 4])
@@ -124,18 +126,22 @@ def tile_qwen2decoderlayer_pa_t_kernel(
         w_codes = consts.tile([P, 3 * HD], U32, align_bytes=64)
         w_scales = consts.tile([P, 3 * HD], U8, align_bytes=64)
 
+        wT_of = []
+        for head in range(3):
+            wT_ps = psum.tile([P, 2, HD], F32, tag="acc_qk" if head == 2 else "back_qk")
+            for half in range(2):
+                nc.tensor.transpose(
+                    wT_ps[:, half, :],
+                    w_rows[:, head, :].bitcast(F32)[:, half : 2 * P : 2],
+                    ident_f32[:],
+                )
+            wT_of.append(wT_ps)
+
         def prepare_weights():
             for head in range(3):
-                wT_ps = psum.tile([P, 2, HD], F32, tag="back_qk")
-                for half in range(2):
-                    nc.tensor.transpose(
-                        wT_ps[:, half, :],
-                        w_rows[:, head, :].bitcast(F32)[:, half : 2 * P : 2],
-                        ident_f32[:],
-                    )
                 nc.vector.tensor_copy(
                     out=w_grouped[:, head, :].bitcast(F32).rearrange("p (d h) -> p d h", h=2),
-                    in_=wT_ps[:].rearrange("p h d -> p d h"),
+                    in_=wT_of[head][:].rearrange("p h d -> p d h"),
                 )
             for head in range(3):
                 cols = slice(head * HD, (head + 1) * HD)
@@ -148,7 +154,7 @@ def tile_qwen2decoderlayer_pa_t_kernel(
         x_ss_of, x_rstd_of, h_of, hT_of, grouped_of = {}, {}, {}, {}, {}
         codes_of, scales_of, acc_qk_of, v_ps_of, back_of = {}, {}, {}, {}, {}
         gainedT_of, squaredT_of, head_ss_of, head_rstd_of = {}, {}, {}, {}
-        direct_of, crossed_of = {}, {}
+        products_of = {}
 
         def x_sum_of_squares(u):
             x_ss = small.tile([P, TILES], F32)
@@ -278,43 +284,34 @@ def tile_qwen2decoderlayer_pa_t_kernel(
             )
             head_rstd_of[u] = rstd
 
-        def rope_products(u):
-            both = [P, 2, TILES, HD]
-            direct = work.tile(both, F32)
-            crossed = work.tile(both, F32)
-            for head in range(2):
+        def rope_products(u, heads):
+            if 0 in heads:
+                products_of[u] = work.tile([P, 2, TILES, 2, HD], F32, name="products")
+            for head in heads:
                 for j in range(TILES):
-                    rstd = head_rstd_of[u][:, head, j : j + 1]
                     nc.vector.scalar_tensor_tensor(
-                        out=direct[:, head, j, :], in0=back_of[u][:, head, j, :], scalar=rstd,
-                        in1=cos_of[u][:, j, :], op0=ALU.mult, op1=ALU.mult,
-                    )
-                    nc.vector.scalar_tensor_tensor(
-                        out=crossed[:, head, j, :].rearrange("p (s d) -> p s d", s=2),
-                        in0=back_of[u][:, head, j, :].rearrange("p (s d) -> p s d", s=2)[:, ::-1, :],
-                        scalar=rstd,
-                        in1=sin_of[u][:, j, :].rearrange("p (s d) -> p s d", s=2),
+                        out=products_of[u][:, head, j, :, :],
+                        in0=back_of[u][:, head, j, :].unsqueeze(1).to_broadcast([P, 2, HD]),
+                        scalar=head_rstd_of[u][:, head, j : j + 1],
+                        in1=angles_of[u][:, j, :].rearrange("p (s d) -> p s d", s=2),
                         op0=ALU.mult, op1=ALU.mult,
                     )
-            direct_of[u], crossed_of[u] = direct, crossed
 
-        def rope_sum(u):
-            direct, crossed = direct_of[u], crossed_of[u]
+        def rope_sum(u, heads, engine):
             lo, hi = slice(0, HALF), slice(HALF, HD)
-            qk_sb = results.tile([P, 2, TILES, HD], F32)
-            for here, op in ((lo, ALU.subtract), (hi, ALU.add)):
-                nc.gpsimd.tensor_tensor(
-                    out=qk_sb[:, :, :, here], in0=direct[:, :, :, here],
-                    in1=crossed[:, :, :, here], op=op,
+            products = products_of[u][:, heads[0] : heads[-1] + 1, :, :, :]
+            qk_sb = results.tile([P, len(heads), TILES, HD], F32, name="qk_%d" % len(heads))
+            for here, there, op in ((lo, hi, ALU.subtract), (hi, lo, ALU.add)):
+                engine.tensor_tensor(
+                    out=qk_sb[:, :, :, here], in0=products[:, :, :, 0, here],
+                    in1=products[:, :, :, 1, there], op=op,
                 )
             rows = slice(u * UNIT, (u + 1) * UNIT)
-            for head, out in enumerate((q_out, k_out)):
+            for i, head in enumerate(heads):
                 nc.sync.dma_start(
-                    out=out[rows, :].rearrange("(p j) d -> p j d", j=TILES),
-                    in_=qk_sb[:, head, :, :],
+                    out=(q_out, k_out)[head][rows, :].rearrange("(p j) d -> p j d", j=TILES),
+                    in_=qk_sb[:, i, :, :],
                 )
-
-        prepare_weights()
 
         def live(u):
             return 0 <= u < N_UNITS
@@ -345,6 +342,13 @@ def tile_qwen2decoderlayer_pa_t_kernel(
             if live(r - 1):
                 first_norm(r - 1)
                 h_transposes(r - 1)
-            if live(r - 5):
-                rope_products(r - 5)
-                rope_sum(r - 5)
+            if r == WEIGHTS_ROUND:
+                prepare_weights()
+            if live(r - 5) and r - 5 < N_UNITS - 1:
+                rope_products(r - 5, (0, 1))
+                rope_sum(r - 5, (0, 1), nc.gpsimd)
+            elif live(r - 5):
+                rope_products(r - 5, (0,))
+                rope_sum(r - 5, (0,), nc.gpsimd)
+                rope_products(r - 5, (1,))
+                rope_sum(r - 5, (1,), nc.vector)

@@ -174,23 +174,27 @@ def tile_qwen2decoderlayer_pa_t_kernel(
             )
             x_rstd_of[u] = rstd
 
+        def by_words(features):
+            return features.rearrange("p (w s e) -> p s w e", s=2, e=2)
+
         def first_norm(u):
-            h_sb = work.tile([P, TILES, HID], BF16)
+            h_sb = work.tile([P, TILES, 2, 2 * P], BF16)
             for j in range(TILES):
-                nc.vector.scalar_tensor_tensor(
-                    out=h_sb[:, j, :], in0=x_of[u][:, j, :], scalar=x_rstd_of[u][:, j : j + 1],
-                    in1=ln1_gain[:], op0=ALU.mult, op1=ALU.mult,
-                )
+                for s in range(2):
+                    nc.vector.scalar_tensor_tensor(
+                        out=h_sb[:, j, s, :].rearrange("p (w e) -> p w e", e=2),
+                        in0=by_words(x_of[u][:, j, :])[:, s, :, :],
+                        scalar=x_rstd_of[u][:, j : j + 1],
+                        in1=by_words(ln1_gain[:])[:, s, :, :], op0=ALU.mult, op1=ALU.mult,
+                    )
             h_of[u] = h_sb
 
         def h_transposes(u):
             hT_ps = psum.tile([P, TILES, 2, P], F32, bufs=1)
             for j in range(TILES):
-                for half in range(2):
+                for s in range(2):
                     nc.tensor.transpose(
-                        hT_ps[:, j, half, :],
-                        h_of[u][:, j, :].bitcast(F32)[:, half : 2 * P : 2],
-                        ident_f32[:],
+                        hT_ps[:, j, s, :], h_of[u][:, j, s, :].bitcast(F32), ident_f32[:]
                     )
             hT_of[u] = hT_ps
 
@@ -248,14 +252,26 @@ def tile_qwen2decoderlayer_pa_t_kernel(
             squaredT = work.tile([P, 2, UNIT], F32)
             for head in range(2):
                 nc.scalar.activation(
-                    out=gainedT[:, head, :], in_=acc_qk_of[u][:, head, :], func=ACT.Identity,
-                    scale=gain_col[:, head : head + 1], bias=gained_bias_col[:, head : head + 1],
-                )
-                nc.scalar.activation(
                     out=squaredT[:, head, :], in_=acc_qk_of[u][:, head, :], func=ACT.Square,
                     bias=bias_col[:, head : head + 1],
                 )
+            for head in range(2):
+                nc.scalar.activation(
+                    out=gainedT[:, head, :], in_=acc_qk_of[u][:, head, :], func=ACT.Identity,
+                    scale=gain_col[:, head : head + 1], bias=gained_bias_col[:, head : head + 1],
+                )
             gainedT_of[u], squaredT_of[u] = gainedT, squaredT
+
+        def sum_squares(u):
+            head_ss = psum.tile([P, 2, TILES, SUM_COLS], F32, bufs=1)
+            for head in range(2):
+                for j in range(TILES):
+                    nc.tensor.matmul(
+                        out=head_ss[:, head, j, :],
+                        lhsT=squaredT_of[u][:, head, j * P : (j + 1) * P], rhs=ones[:],
+                        start=True, stop=True,
+                    )
+            head_ss_of[u] = head_ss
 
         def turn_back(u):
             back_qk = psum.tile([P, 2, TILES, HD], F32)
@@ -266,15 +282,6 @@ def tile_qwen2decoderlayer_pa_t_kernel(
                         ident_f32[:],
                     )
             back_of[u] = back_qk
-            head_ss = psum.tile([P, 2, TILES, SUM_COLS], F32, bufs=1)
-            for head in range(2):
-                for j in range(TILES):
-                    nc.tensor.matmul(
-                        out=head_ss[:, head, j, :],
-                        lhsT=squaredT_of[u][:, head, j * P : (j + 1) * P], rhs=ones[:],
-                        start=True, stop=True,
-                    )
-            head_ss_of[u] = head_ss
 
         def head_rstd(u):
             rstd = small.tile([P, 2, TILES], F32, name="head_rstd_sb")
@@ -332,6 +339,7 @@ def tile_qwen2decoderlayer_pa_t_kernel(
             if live(r - 5):
                 head_rstd(r - 5)
             if live(r - 4):
+                sum_squares(r - 4)
                 turn_back(r - 4)
             if live(r):
                 x_sum_of_squares(r)

@@ -20,9 +20,12 @@ EPS = 1e-6
 TILES = 2
 UNIT = TILES * P
 N_UNITS = TOKENS // UNIT
+PAIR = 2
+PAIR_TILES = PAIR * TILES
+N_PAIRS = N_UNITS // PAIR
 DEPTH = 5
 WEIGHTS_ROUND = 1
-LOAD_AHEAD = 8
+LOAD_AHEAD = 4
 GAIN_ROWS = HID // P
 SUM_COLS = 64
 
@@ -40,37 +43,48 @@ def tile_qwen2decoderlayer_pa_t_kernel(
     with ExitStack() as ctx:
         ctx.enter_context(tc.manual_schedule())
         consts = ctx.enter_context(tc.tile_pool(name="consts", bufs=1))
-        inputs = ctx.enter_context(tc.tile_pool(name="inputs", bufs=N_UNITS))
+        inputs = ctx.enter_context(tc.tile_pool(name="inputs", bufs=N_PAIRS))
         work = ctx.enter_context(tc.tile_pool(name="work", bufs=3))
         small = ctx.enter_context(tc.tile_pool(name="small", bufs=4))
         unread = ctx.enter_context(tc.tile_pool(name="unread", bufs=4))
         results = ctx.enter_context(tc.tile_pool(name="results", bufs=6))
         psum = ctx.enter_context(tc.psum_pool(name="psum", bufs=2))
 
-        x_of, angles_of = {}, {}
+        x_pair_of, x_of, angles_of = {}, {}, {}
 
-        def load_x(u):
-            x_sb = inputs.tile([P, TILES, HID], BF16)
+        def tokens_of(pair):
+            return slice(pair * PAIR * UNIT, (pair + 1) * PAIR * UNIT)
+
+        def tiles_of(u):
+            return slice(u % PAIR * TILES, (u % PAIR + 1) * TILES)
+
+        def load_x(pair, units=(0, PAIR)):
+            if units[0] == 0:
+                x_pair_of[pair] = inputs.tile([P, PAIR_TILES, HID], BF16, name="x_pair")
+            tiles = slice(units[0] * TILES, units[1] * TILES)
             nc.sync.dma_start(
-                out=x_sb[:],
-                in_=x[u * UNIT : (u + 1) * UNIT, :].rearrange("(p j) k -> p j k", j=TILES),
+                out=x_pair_of[pair][:, tiles, :],
+                in_=x[tokens_of(pair), :].rearrange("(p j) k -> p j k", j=PAIR_TILES)[:, tiles, :],
             )
-            x_of[u] = x_sb
+            for i in range(*units):
+                x_of[pair * PAIR + i] = x_pair_of[pair][:, tiles_of(i), :]
 
-        def load_angles(u):
-            rows = slice(u * UNIT, (u + 1) * UNIT)
-            angles = inputs.tile([P, TILES, 2 * HD], BF16)
+        def load_angles(pair):
+            angles = inputs.tile([P, PAIR_TILES, 2 * HD], BF16)
             for first, table, columns in (
                 (0, cos, slice(0, HD)), (HD, sin, slice(HALF, HD)), (HD + HALF, sin, slice(0, HALF))
             ):
                 width = columns.stop - columns.start
                 nc.sync.dma_start(
                     out=angles[:, :, first : first + width],
-                    in_=table[rows, columns].rearrange("(p j) d -> p j d", j=TILES),
+                    in_=table[tokens_of(pair), columns].rearrange(
+                        "(p j) d -> p j d", j=PAIR_TILES
+                    ),
                 )
-            angles_of[u] = angles
+            for i in range(PAIR):
+                angles_of[pair * PAIR + i] = angles[:, tiles_of(i), :]
 
-        load_x(0)
+        load_x(0, (0, 1))
         vector_rows = consts.tile([P, P], BF16)
         nc.vector.memset(vector_rows[:], 0.0)
         nc.sync.dma_start(
@@ -81,17 +95,17 @@ def tile_qwen2decoderlayer_pa_t_kernel(
                 out=vector_rows[GAIN_ROWS + row : GAIN_ROWS + row + 1, :],
                 in_=vec.rearrange("(o d) -> o d", o=1),
             )
-        load_x(1)
+        load_x(0, (1, 2))
         w_rows = consts.tile([P, 3, HID], BF16)
         for head, w in enumerate((wq, wk, wv)):
             nc.sync.dma_start(out=w_rows[:, head, :], in_=w)
-        load_x(2)
+        load_x(1, (0, 1))
+        load_x(1, (1, 2))
         v_bias = consts.tile([P, HD], BF16)
         nc.sync.dma_start(out=v_bias[:], in_=bv.partition_broadcast(P))
-        for u in range(LOAD_AHEAD):
-            if u + 3 < N_UNITS:
-                load_x(u + 3)
-            load_angles(u)
+        for pair in range(LOAD_AHEAD):
+            load_x(pair + 2)
+            load_angles(pair)
 
         eps_col = consts.tile([P, 1], F32)
         nc.vector.memset(eps_col[:], EPS)
@@ -152,9 +166,9 @@ def tile_qwen2decoderlayer_pa_t_kernel(
                 )
 
         x_ss_of, x_rstd_of, h_of, hT_of, grouped_of = {}, {}, {}, {}, {}
-        codes_of, scales_of, acc_qk_of, v_ps_of, back_of = {}, {}, {}, {}, {}
+        codes_of, scales_of, acc_qk_of, v_pair_of, back_of = {}, {}, {}, {}, {}
         gainedT_of, squaredT_of, head_ss_of, head_rstd_of = {}, {}, {}, {}
-        products_of = {}
+        products_of, qk_of = {}, {}
 
         def x_sum_of_squares(u):
             x_ss = small.tile([P, TILES], F32)
@@ -174,27 +188,23 @@ def tile_qwen2decoderlayer_pa_t_kernel(
             )
             x_rstd_of[u] = rstd
 
-        def by_words(features):
-            return features.rearrange("p (w s e) -> p s w e", s=2, e=2)
-
         def first_norm(u):
-            h_sb = work.tile([P, TILES, 2, 2 * P], BF16)
+            h_sb = work.tile([P, TILES, HID], BF16)
             for j in range(TILES):
-                for s in range(2):
-                    nc.vector.scalar_tensor_tensor(
-                        out=h_sb[:, j, s, :].rearrange("p (w e) -> p w e", e=2),
-                        in0=by_words(x_of[u][:, j, :])[:, s, :, :],
-                        scalar=x_rstd_of[u][:, j : j + 1],
-                        in1=by_words(ln1_gain[:])[:, s, :, :], op0=ALU.mult, op1=ALU.mult,
-                    )
+                nc.vector.scalar_tensor_tensor(
+                    out=h_sb[:, j, :], in0=x_of[u][:, j, :], scalar=x_rstd_of[u][:, j : j + 1],
+                    in1=ln1_gain[:], op0=ALU.mult, op1=ALU.mult,
+                )
             h_of[u] = h_sb
 
         def h_transposes(u):
             hT_ps = psum.tile([P, TILES, 2, P], F32, bufs=1)
             for j in range(TILES):
-                for s in range(2):
+                for half in range(2):
                     nc.tensor.transpose(
-                        hT_ps[:, j, s, :], h_of[u][:, j, s, :].bitcast(F32), ident_f32[:]
+                        hT_ps[:, j, half, :],
+                        h_of[u][:, j, :].bitcast(F32)[:, half : 2 * P : 2],
+                        ident_f32[:],
                     )
             hT_of[u] = hT_ps
 
@@ -224,7 +234,9 @@ def tile_qwen2decoderlayer_pa_t_kernel(
                     rhs=codes_of[u][:].bitcast(FP8X4), rhs_scale=scales_of[u][:],
                     start=True, stop=True,
                 )
-            v_ps = psum.tile([P, TILES, HD], F32, bufs=1)
+            if u % PAIR == 0:
+                v_pair_of[u // PAIR] = psum.tile([P, PAIR, TILES, HD], F32, bufs=1, name="v_pair")
+            v_ps = v_pair_of[u // PAIR][:, u % PAIR, :, :]
             v_cols = slice(2 * HD, 3 * HD)
             for j in range(TILES):
                 tok = slice(j * P, (j + 1) * P)
@@ -234,16 +246,16 @@ def tile_qwen2decoderlayer_pa_t_kernel(
                     rhs=w_codes[:, v_cols].bitcast(FP8X4), rhs_scale=w_scales[:, v_cols],
                     start=True, stop=True,
                 )
-            acc_qk_of[u], v_ps_of[u] = acc_qk, v_ps
+            acc_qk_of[u] = acc_qk
 
-        def finish_v(u):
-            v_sb = results.tile([P, TILES, HD], F32)
+        def finish_v(pair):
+            v_sb = results.tile([P, PAIR_TILES, HD], F32)
             nc.vector.tensor_tensor(
-                out=v_sb[:], in0=v_ps_of[u][:],
-                in1=v_bias[:].unsqueeze(1).to_broadcast([P, TILES, HD]), op=ALU.add,
+                out=v_sb[:], in0=v_pair_of[pair][:].rearrange("p u j d -> p (u j) d"),
+                in1=v_bias[:].unsqueeze(1).to_broadcast([P, PAIR_TILES, HD]), op=ALU.add,
             )
             nc.sync.dma_start(
-                out=v_out[u * UNIT : (u + 1) * UNIT, :].rearrange("(p j) d -> p j d", j=TILES),
+                out=v_out[tokens_of(pair), :].rearrange("(p j) d -> p j d", j=PAIR_TILES),
                 in_=v_sb[:],
             )
 
@@ -306,32 +318,37 @@ def tile_qwen2decoderlayer_pa_t_kernel(
 
         def rope_sum(u, heads, engine):
             lo, hi = slice(0, HALF), slice(HALF, HD)
-            products = products_of[u][:, heads[0] : heads[-1] + 1, :, :, :]
-            qk_sb = results.tile([P, len(heads), TILES, HD], F32, name="qk_%d" % len(heads))
+            if u % PAIR == 0:
+                qk_of[u // PAIR] = results.tile([P, 2, PAIR_TILES, HD], F32, name="qk")
+            pick = slice(heads[0], heads[-1] + 1)
+            qk, products = qk_of[u // PAIR][:, pick, tiles_of(u), :], products_of[u]
             for here, there, op in ((lo, hi, ALU.subtract), (hi, lo, ALU.add)):
                 engine.tensor_tensor(
-                    out=qk_sb[:, :, :, here], in0=products[:, :, :, 0, here],
-                    in1=products[:, :, :, 1, there], op=op,
+                    out=qk[:, :, :, here], in0=products[:, pick, :, 0, here],
+                    in1=products[:, pick, :, 1, there], op=op,
                 )
-            rows = slice(u * UNIT, (u + 1) * UNIT)
-            for i, head in enumerate(heads):
+
+        def store_qk(pair, heads, tiles):
+            for head in heads:
                 nc.sync.dma_start(
-                    out=(q_out, k_out)[head][rows, :].rearrange("(p j) d -> p j d", j=TILES),
-                    in_=qk_sb[:, i, :, :],
+                    out=(q_out, k_out)[head][tokens_of(pair), :].rearrange(
+                        "(p j) d -> p j d", j=PAIR_TILES
+                    )[:, tiles, :],
+                    in_=qk_of[pair][:, head, tiles, :],
                 )
 
         def live(u):
             return 0 <= u < N_UNITS
 
         for r in range(N_UNITS + DEPTH):
-            if r + LOAD_AHEAD + 3 < N_UNITS:
-                load_x(r + LOAD_AHEAD + 3)
-            if r + LOAD_AHEAD < N_UNITS:
-                load_angles(r + LOAD_AHEAD)
+            if r % PAIR == 0 and r // PAIR + LOAD_AHEAD + 2 < N_PAIRS:
+                load_x(r // PAIR + LOAD_AHEAD + 2)
+            if r % PAIR == 0 and r // PAIR + LOAD_AHEAD < N_PAIRS:
+                load_angles(r // PAIR + LOAD_AHEAD)
             if live(r - 3):
                 h_quantise(r - 3)
-            if live(r - 4):
-                finish_v(r - 4)
+            if live(r - 4) and (r - 4) % PAIR == PAIR - 1:
+                finish_v((r - 4) // PAIR)
             if live(r - 3):
                 projections(r - 3)
             if live(r - 4):
@@ -355,8 +372,12 @@ def tile_qwen2decoderlayer_pa_t_kernel(
             if live(r - 5) and r - 5 < N_UNITS - 1:
                 rope_products(r - 5, (0, 1))
                 rope_sum(r - 5, (0, 1), nc.gpsimd)
+                if r - 5 == N_UNITS - PAIR:
+                    store_qk(N_PAIRS - 1, (0, 1), tiles_of(r - 5))
+                elif (r - 5) % PAIR == PAIR - 1:
+                    store_qk((r - 5) // PAIR, (0, 1), slice(0, PAIR_TILES))
             elif live(r - 5):
-                rope_products(r - 5, (0,))
-                rope_sum(r - 5, (0,), nc.gpsimd)
-                rope_products(r - 5, (1,))
-                rope_sum(r - 5, (1,), nc.vector)
+                for head, engine in ((0, nc.gpsimd), (1, nc.vector)):
+                    rope_products(r - 5, (head,))
+                    rope_sum(r - 5, (head,), engine)
+                    store_qk(N_PAIRS - 1, (head,), tiles_of(r - 5))

from contextlib import ExitStack

import concourse.mybir as mybir
from concourse.masks import make_identity

F32 = mybir.dt.float32
BF16 = mybir.dt.bfloat16
U32 = mybir.dt.uint32
U8 = mybir.dt.uint8
FP8X4 = mybir.dt.float8_e4m3fn_x4
ALU = mybir.AluOpType
ACT = mybir.ActivationFunctionType

P = 128
TOKENS = 8192
HID = 512
HD = 128
HALF = HD // 2
EPS = 1e-6
TILES = 2
UNIT = TILES * P
N_UNITS = TOKENS // UNIT
PAIR = 2
PAIR_TILES = PAIR * TILES
N_PAIRS = N_UNITS // PAIR
DEPTH = 5
WEIGHTS_ROUND = 1
LOAD_AHEAD = 4
GAIN_ROWS = HID // P
SUM_COLS = 64

FLOPS = 2 * TOKENS * HID * 3 * HD


def tile_qwen2decoderlayer_pa_t_kernel(
    tc, x, cos, sin, wq, bq, wk, bk, wv, bv, q_norm_w, k_norm_w, ln1_w, out_0, out_1, out_2
):
    nc = tc.nc
    q_out = out_0.flatten_outer_dims()
    k_out = out_1.flatten_outer_dims()
    v_out = out_2.flatten_outer_dims()

    with ExitStack() as ctx:
        ctx.enter_context(tc.manual_schedule())
        consts = ctx.enter_context(tc.tile_pool(name="consts", bufs=1))
        inputs = ctx.enter_context(tc.tile_pool(name="inputs", bufs=N_PAIRS))
        work = ctx.enter_context(tc.tile_pool(name="work", bufs=3))
        small = ctx.enter_context(tc.tile_pool(name="small", bufs=4))
        unread = ctx.enter_context(tc.tile_pool(name="unread", bufs=4))
        results = ctx.enter_context(tc.tile_pool(name="results", bufs=6))
        psum = ctx.enter_context(tc.psum_pool(name="psum", bufs=2))

        x_pair_of, x_of, angles_of = {}, {}, {}

        def tokens_of(pair):
            return slice(pair * PAIR * UNIT, (pair + 1) * PAIR * UNIT)

        def tiles_of(u):
            return slice(u % PAIR * TILES, (u % PAIR + 1) * TILES)

        def load_x(pair, units=(0, PAIR)):
            if units[0] == 0:
                x_pair_of[pair] = inputs.tile([P, PAIR_TILES, HID], BF16, name="x_pair")
            tiles = slice(units[0] * TILES, units[1] * TILES)
            nc.sync.dma_start(
                out=x_pair_of[pair][:, tiles, :],
                in_=x[tokens_of(pair), :].rearrange("(p j) k -> p j k", j=PAIR_TILES)[:, tiles, :],
            )
            for i in range(*units):
                x_of[pair * PAIR + i] = x_pair_of[pair][:, tiles_of(i), :]

        def load_angles(pair):
            angles = inputs.tile([P, PAIR_TILES, 2 * HD], BF16)
            for first, table, columns in (
                (0, cos, slice(0, HD)), (HD, sin, slice(HALF, HD)), (HD + HALF, sin, slice(0, HALF))
            ):
                width = columns.stop - columns.start
                nc.sync.dma_start(
                    out=angles[:, :, first : first + width],
                    in_=table[tokens_of(pair), columns].rearrange(
                        "(p j) d -> p j d", j=PAIR_TILES
                    ),
                )
            for i in range(PAIR):
                angles_of[pair * PAIR + i] = angles[:, tiles_of(i), :]

        load_x(0, (0, 1))
        vector_rows = consts.tile([P, P], BF16)
        nc.vector.memset(vector_rows[:], 0.0)
        nc.sync.dma_start(
            out=vector_rows[0:GAIN_ROWS, :], in_=ln1_w.rearrange("(c k) -> c k", c=GAIN_ROWS)
        )
        for row, vec in enumerate((bq, bk, q_norm_w, k_norm_w)):
            nc.sync.dma_start(
                out=vector_rows[GAIN_ROWS + row : GAIN_ROWS + row + 1, :],
                in_=vec.rearrange("(o d) -> o d", o=1),
            )
        load_x(0, (1, 2))
        w_rows = consts.tile([P, 3, HID], BF16)
        for head, w in enumerate((wq, wk, wv)):
            nc.sync.dma_start(out=w_rows[:, head, :], in_=w)
        load_x(1, (0, 1))
        load_x(1, (1, 2))
        v_bias = consts.tile([P, HD], BF16)
        nc.sync.dma_start(out=v_bias[:], in_=bv.partition_broadcast(P))
        for pair in range(LOAD_AHEAD):
            load_x(pair + 2)
            load_angles(pair)

        eps_col = consts.tile([P, 1], F32)
        nc.vector.memset(eps_col[:], EPS)
        first_root = consts.tile([P, 1], F32)
        nc.scalar.activation(out=first_root[:], in_=eps_col[:], func=ACT.Abs_reciprocal_sqrt)
        ident_f32 = consts.tile([P, P], F32)
        make_identity(nc, ident_f32[:])
        ident_bf16 = consts.tile([P, P], BF16)
        make_identity(nc, ident_bf16[:])

        vectorsT_ps = psum.tile([P, P], BF16, tag="acc_qk")
        nc.tensor.transpose(vectorsT_ps[:], vector_rows[:], ident_bf16[:])
        vector_cols = consts.tile([P, GAIN_ROWS + 4], F32)
        nc.vector.tensor_copy(out=vector_cols[:], in_=vectorsT_ps[:, 0 : GAIN_ROWS + 4])
        bias_col = vector_cols[:, GAIN_ROWS : GAIN_ROWS + 2]
        gain_col = vector_cols[:, GAIN_ROWS + 2 : GAIN_ROWS + 4]
        gained_bias_col = consts.tile([P, 2], F32)
        nc.vector.tensor_tensor(
            out=gained_bias_col[:], in0=bias_col, in1=gain_col, op=ALU.mult
        )
        ones = consts.tile([P, SUM_COLS], F32)
        nc.vector.memset(ones[:], 1.0)
        ln1_gain = psum.tile([P, HID], F32, bufs=1)
        for c in range(GAIN_ROWS):
            nc.tensor.transpose(
                ln1_gain[:, c * P : (c + 1) * P],
                vector_cols[:, c : c + 1].to_broadcast([P, P]),
                ident_f32[:],
            )

        w_grouped = consts.tile([P, 3, HID], BF16, align_bytes=64)
        w_codes = consts.tile([P, 3 * HD], U32, align_bytes=64)
        w_scales = consts.tile([P, 3 * HD], U8, align_bytes=64)

        wT_of = []
        for head in range(3):
            wT_ps = psum.tile([P, 2, HD], F32, tag="acc_qk" if head == 2 else "back_qk")
            for half in range(2):
                nc.tensor.transpose(
                    wT_ps[:, half, :],
                    w_rows[:, head, :].bitcast(F32)[:, half : 2 * P : 2],
                    ident_f32[:],
                )
            wT_of.append(wT_ps)

        def prepare_weights():
            for head in range(3):
                nc.vector.tensor_copy(
                    out=w_grouped[:, head, :].bitcast(F32).rearrange("p (d h) -> p d h", h=2),
                    in_=wT_of[head][:].rearrange("p h d -> p d h"),
                )
            for head in range(3):
                cols = slice(head * HD, (head + 1) * HD)
                nc.vector.quantize_mx(
                    out=w_codes[:, cols].bitcast(FP8X4),
                    scales=w_scales[:, cols],
                    in_=w_grouped[:, head, :],
                )

        x_ss_of, x_rstd_of, h_of, hT_of, grouped_of = {}, {}, {}, {}, {}
        codes_of, scales_of, acc_qk_of, v_pair_of, back_of = {}, {}, {}, {}, {}
        gainedT_of, squaredT_of, head_ss_of, head_rstd_of = {}, {}, {}, {}
        products_of, qk_of = {}, {}

        def x_sum_of_squares(u):
            x_ss = small.tile([P, TILES], F32)
            for j in range(TILES):
                x_sq = unread.tile([P, HID], BF16)
                nc.scalar.activation(
                    out=x_sq[:], in_=x_of[u][:, j, :], func=ACT.Square,
                    accum_out=x_ss[:, j : j + 1],
                )
            x_ss_of[u] = x_ss

        def x_rstd(u):
            rstd = small.tile([P, TILES], F32, name="x_rstd_sb")
            nc.scalar.activation(
                out=rstd[:], in_=x_ss_of[u][:], func=ACT.Abs_reciprocal_sqrt, bias=eps_col[:],
                scale=1.0 / HID,
            )
            x_rstd_of[u] = rstd

        def first_norm(u):
            h_sb = work.tile([P, TILES, HID], BF16)
            for j in range(TILES):
                nc.vector.scalar_tensor_tensor(
                    out=h_sb[:, j, :], in0=x_of[u][:, j, :], scalar=x_rstd_of[u][:, j : j + 1],
                    in1=ln1_gain[:], op0=ALU.mult, op1=ALU.mult,
                )
            h_of[u] = h_sb

        def h_transposes(u):
            hT_ps = psum.tile([P, TILES, 2, P], F32, bufs=1)
            for j in range(TILES):
                for half in range(2):
                    nc.tensor.transpose(
                        hT_ps[:, j, half, :],
                        h_of[u][:, j, :].bitcast(F32)[:, half : 2 * P : 2],
                        ident_f32[:],
                    )
            hT_of[u] = hT_ps

        def h_regroup(u):
            h_grouped = work.tile([P, UNIT * 4], BF16, align_bytes=64)
            nc.scalar.copy(
                out=h_grouped[:].bitcast(F32).rearrange("p (j t h) -> p j t h", j=TILES, h=2),
                in_=hT_of[u][:].rearrange("p j h t -> p j t h"),
            )
            grouped_of[u] = h_grouped

        def h_quantise(u):
            h_codes = work.tile([P, UNIT], U32, align_bytes=64)
            h_scales = work.tile([P, UNIT], U8, align_bytes=64)
            nc.vector.quantize_mx(
                out=h_codes[:].bitcast(FP8X4), scales=h_scales[:], in_=grouped_of[u][:]
            )
            codes_of[u], scales_of[u] = h_codes, h_scales

        def projections(u):
            acc_qk = psum.tile([P, 2, UNIT], F32)
            for head in range(2):
                cols = slice(head * HD, (head + 1) * HD)
                nc.tensor.matmul_mx(
                    out=acc_qk[:, head, :],
                    lhsT=w_codes[:, cols].bitcast(FP8X4), lhsT_scale=w_scales[:, cols],
                    rhs=codes_of[u][:].bitcast(FP8X4), rhs_scale=scales_of[u][:],
                    start=True, stop=True,
                )
            if u % PAIR == 0:
                v_pair_of[u // PAIR] = psum.tile([P, PAIR, TILES, HD], F32, bufs=1, name="v_pair")
            v_ps = v_pair_of[u // PAIR][:, u % PAIR, :, :]
            v_cols = slice(2 * HD, 3 * HD)
            for j in range(TILES):
                tok = slice(j * P, (j + 1) * P)
                nc.tensor.matmul_mx(
                    out=v_ps[:, j, :],
                    lhsT=codes_of[u][:, tok].bitcast(FP8X4), lhsT_scale=scales_of[u][:, tok],
                    rhs=w_codes[:, v_cols].bitcast(FP8X4), rhs_scale=w_scales[:, v_cols],
                    start=True, stop=True,
                )
            acc_qk_of[u] = acc_qk

        def finish_v(pair):
            v_sb = results.tile([P, PAIR_TILES, HD], F32)
            nc.vector.tensor_tensor(
                out=v_sb[:], in0=v_pair_of[pair][:].rearrange("p u j d -> p (u j) d"),
                in1=v_bias[:].unsqueeze(1).to_broadcast([P, PAIR_TILES, HD]), op=ALU.add,
            )
            nc.sync.dma_start(
                out=v_out[tokens_of(pair), :].rearrange("(p j) d -> p j d", j=PAIR_TILES),
                in_=v_sb[:],
            )

        def heads_out_of_psum(u):
            gainedT = work.tile([P, 2, UNIT], F32)
            squaredT = work.tile([P, 2, UNIT], F32)
            for head in range(2):
                nc.scalar.activation(
                    out=squaredT[:, head, :], in_=acc_qk_of[u][:, head, :], func=ACT.Square,
                    bias=bias_col[:, head : head + 1],
                )
            for head in range(2):
                nc.scalar.activation(
                    out=gainedT[:, head, :], in_=acc_qk_of[u][:, head, :], func=ACT.Identity,
                    scale=gain_col[:, head : head + 1], bias=gained_bias_col[:, head : head + 1],
                )
            gainedT_of[u], squaredT_of[u] = gainedT, squaredT

        def sum_squares(u):
            head_ss = psum.tile([P, 2, TILES, SUM_COLS], F32, bufs=1)
            for head in range(2):
                for j in range(TILES):
                    nc.tensor.matmul(
                        out=head_ss[:, head, j, :],
                        lhsT=squaredT_of[u][:, head, j * P : (j + 1) * P], rhs=ones[:],
                        start=True, stop=True,
                    )
            head_ss_of[u] = head_ss

        def turn_back(u):
            back_qk = psum.tile([P, 2, TILES, HD], F32)
            for head in range(2):
                for j in range(TILES):
                    nc.tensor.transpose(
                        back_qk[:, head, j, :], gainedT_of[u][:, head, j * P : (j + 1) * P],
                        ident_f32[:],
                    )
            back_of[u] = back_qk

        def head_rstd(u):
            rstd = small.tile([P, 2, TILES], F32, name="head_rstd_sb")
            nc.scalar.activation(
                out=rstd[:], in_=head_ss_of[u][:, :, :, 0], func=ACT.Abs_reciprocal_sqrt,
                bias=eps_col[:], scale=1.0 / HD,
            )
            head_rstd_of[u] = rstd

        def rope_products(u, heads):
            if 0 in heads:
                products_of[u] = work.tile([P, 2, TILES, 2, HD], F32, name="products")
            for head in heads:
                for j in range(TILES):
                    nc.vector.scalar_tensor_tensor(
                        out=products_of[u][:, head, j, :, :],
                        in0=back_of[u][:, head, j, :].unsqueeze(1).to_broadcast([P, 2, HD]),
                        scalar=head_rstd_of[u][:, head, j : j + 1],
                        in1=angles_of[u][:, j, :].rearrange("p (s d) -> p s d", s=2),
                        op0=ALU.mult, op1=ALU.mult,
                    )

        def rope_sum(u, heads, engine):
            lo, hi = slice(0, HALF), slice(HALF, HD)
            if u % PAIR == 0:
                qk_of[u // PAIR] = results.tile([P, 2, PAIR_TILES, HD], F32, name="qk")
            pick = slice(heads[0], heads[-1] + 1)
            qk, products = qk_of[u // PAIR][:, pick, tiles_of(u), :], products_of[u]
            for here, there, op in ((lo, hi, ALU.subtract), (hi, lo, ALU.add)):
                engine.tensor_tensor(
                    out=qk[:, :, :, here], in0=products[:, pick, :, 0, here],
                    in1=products[:, pick, :, 1, there], op=op,
                )

        def store_qk(pair, heads, tiles):
            for head in heads:
                nc.sync.dma_start(
                    out=(q_out, k_out)[head][tokens_of(pair), :].rearrange(
                        "(p j) d -> p j d", j=PAIR_TILES
                    )[:, tiles, :],
                    in_=qk_of[pair][:, head, tiles, :],
                )

        def live(u):
            return 0 <= u < N_UNITS

        for r in range(N_UNITS + DEPTH):
            if r % PAIR == 0 and r // PAIR + LOAD_AHEAD + 2 < N_PAIRS:
                load_x(r // PAIR + LOAD_AHEAD + 2)
            if r % PAIR == 0 and r // PAIR + LOAD_AHEAD < N_PAIRS:
                load_angles(r // PAIR + LOAD_AHEAD)
            if live(r - 3):
                h_quantise(r - 3)
            if live(r - 4) and (r - 4) % PAIR == PAIR - 1:
                finish_v((r - 4) // PAIR)
            if live(r - 3):
                projections(r - 3)
            if live(r - 4):
                heads_out_of_psum(r - 4)
            if live(r - 5):
                head_rstd(r - 5)
            if live(r - 4):
                sum_squares(r - 4)
                turn_back(r - 4)
            if live(r):
                x_sum_of_squares(r)
            if live(r - 2):
                h_regroup(r - 2)
            if live(r):
                x_rstd(r)
            if live(r - 1):
                first_norm(r - 1)
                h_transposes(r - 1)
            if r == WEIGHTS_ROUND:
                prepare_weights()
            if live(r - 5) and r - 5 < N_UNITS - 1:
                rope_products(r - 5, (0, 1))
                rope_sum(r - 5, (0, 1), nc.gpsimd)
                if r - 5 == N_UNITS - PAIR:
                    store_qk(N_PAIRS - 1, (0, 1), tiles_of(r - 5))
                elif (r - 5) % PAIR == PAIR - 1:
                    store_qk((r - 5) // PAIR, (0, 1), slice(0, PAIR_TILES))
            elif live(r - 5):
                for head, engine in ((0, nc.gpsimd), (1, nc.vector)):
                    rope_products(r - 5, (head,))
                    rope_sum(r - 5, (head,), engine)
                    store_qk(N_PAIRS - 1, (head,), tiles_of(r - 5))
